import numpy as np
import ml_dtypes


def mxq(x, axis, fmt="e4m3"):
    dtype, down = {"e4m3": (ml_dtypes.float8_e4m3fn, 7), "e5m2": (ml_dtypes.float8_e5m2, 14)}[fmt]
    v = np.moveaxis(np.asarray(x, np.float32).astype(ml_dtypes.bfloat16).astype(np.float64), axis, -1)
    blocks = v.reshape(v.shape[:-1] + (-1, 32))
    amax = np.abs(blocks).max(-1, keepdims=True)
    byte = np.maximum(np.where(amax > 0, np.frexp(amax)[1] - 1 + 127, 0) - down, 1)
    scale = np.exp2(byte - 127.0)
    codes = (blocks / scale).astype(np.float32).astype(dtype).astype(np.float64)
    return np.moveaxis((codes * scale).reshape(v.shape), -1, axis)


WIDE = False


def mx_kscale(k):
    if not WIDE:
        return np.ones(k)
    levels = np.array([10, -10, 5, -5, 0])
    a = np.random.permutation(np.resize(levels, k // 512 * 4)).reshape(k // 512, 4)
    idx = np.arange(k)
    return np.exp2(a[idx // 512, idx % 128 // 32])


BF16 = ml_dtypes.bfloat16


def bf(x):
    return np.asarray(x, np.float32).astype(BF16)


def f64(x):
    return np.asarray(x).astype(np.float64)


B, N, D1, D2, F1, F2, F3, F4 = 256, 1, 20480, 20480, 128, 64, 32, 16
K = D1 + D2
EPS = 1e-5
SLOPE = 0.2


def setup_inputs():
    s = mx_kscale(K)
    g = np.sqrt(EPS)
    return {"input1": bf(np.random.standard_normal((B, N, D1)) * s[:D1]),
            "input2": bf(np.random.standard_normal((B, N, D2)) * s[D1:]),
            "W1": bf(np.random.standard_normal((F1, K)) * 5.0 * g / np.sqrt(K) / s[None, :]),
            "b1": bf(np.random.standard_normal(F1) * 2.5 * g)}


def reference(input1, input2, W1, b1):
    x = np.concatenate([f64(input1), f64(input2)], axis=2)
    h = (mxq(x, 2, "e4m3") @ mxq(f64(W1), 1, "e4m3").T) + f64(b1)
    m = h.mean(axis=-1, keepdims=True)
    v = np.square(h - m).mean(axis=-1, keepdims=True)
    hn = (h - m) * (1.0 / np.sqrt(v + EPS))
    return np.where(hn >= 0, hn, SLOPE * hn)

@@ -1,0 +1,178 @@
+from contextlib import ExitStack
+
+import concourse.mybir as mybir
+from concourse.masks import make_identity
+
+F32 = mybir.dt.float32
+BF16 = mybir.dt.bfloat16
+U32 = mybir.dt.uint32
+U8 = mybir.dt.uint8
+FP8X4 = mybir.dt.float8_e4m3fn_x4
+ALU = mybir.AluOpType
+ACT = mybir.ActivationFunctionType
+
+P = 128
+ROW_BLOCKS = 2
+FEATURES = 128
+K_INPUT = 20480
+K_PASS = 512
+PAIRS_PASS = K_PASS // 2
+PASSES_ROUND = 4
+K_ROUND = PASSES_ROUND * K_PASS
+PAIRS_ROUND = K_ROUND // 2
+ROUNDS_INPUT = K_INPUT // K_ROUND
+ROUNDS = 2 * ROUNDS_INPUT
+BANK = 512
+LOAD_BUFS = 8
+EPS = 1e-5
+SLOPE = 0.2
+
+FLOPS = 2 * ROW_BLOCKS * P * FEATURES * 2 * K_INPUT
+
+
+def load_round(nc, raw_pool, input1, input2, W1, j):
+    source = input1 if j < ROUNDS_INPUT else input2
+    k0 = (j % ROUNDS_INPUT) * K_ROUND
+    x_raw = raw_pool.tile([P, ROW_BLOCKS * K_ROUND], BF16, tag="x_raw")
+    w_raw = raw_pool.tile([P, K_ROUND], BF16, tag="w_raw")
+    nc.sync.dma_start(
+        out=x_raw[:].rearrange("p (h k) -> p h k", h=ROW_BLOCKS),
+        in_=source.rearrange("(h p) o k -> p h (o k)", p=P)[:, :, k0 : k0 + K_ROUND],
+    )
+    nc.sync.dma_start(out=w_raw[:], in_=W1[:, j * K_ROUND : (j + 1) * K_ROUND])
+    return x_raw, w_raw
+
+
+def transpose_bank(nc, bank_pool, pairs, starts, ident):
+    bank = bank_pool.tile([P, BANK], F32, tag="bank")
+    for s, start in enumerate(starts):
+        nc.tensor.transpose(bank[:, s * P : (s + 1) * P], pairs[:, start : start + P], ident[:])
+    return bank
+
+
+def bank_by_row(bank):
+    return bank[:].rearrange("p (n u r) -> p n r u", n=2, u=2)
+
+
+def words_by_row(grouped, first_bank):
+    pairs = grouped[:].bitcast(F32)[:, first_bank * BANK : (first_bank + 1) * BANK]
+    return pairs.rearrange("p (n r u) -> p n r u", n=2, u=2)
+
+
+def quantise_half(nc, grouped, codes, scales, half):
+    width = codes.shape[1] // 2
+    cols = slice(half * width, (half + 1) * width)
+    nc.vector.quantize_mx(
+        out=codes[:, cols].bitcast(FP8X4),
+        scales=scales[:, cols],
+        in_=grouped[:, half * width * 4 : (half + 1) * width * 4],
+    )
+
+
+def tile_fcd_pa_kernel(tc, input1, input2, W1, b1, out):
+    nc = tc.nc
+    with ExitStack() as ctx:
+        ctx.enter_context(tc.manual_schedule())
+        const = ctx.enter_context(tc.tile_pool(name="const", bufs=1))
+        raw_pool = ctx.enter_context(tc.tile_pool(name="raw", bufs=LOAD_BUFS))
+        grouped_pool = ctx.enter_context(tc.tile_pool(name="grouped", bufs=2))
+        mx_pool = ctx.enter_context(tc.tile_pool(name="mx", bufs=3))
+        tail = ctx.enter_context(tc.tile_pool(name="tail", bufs=1))
+        bank_pool = ctx.enter_context(tc.psum_pool(name="banks", bufs=6))
+        acc_pool = ctx.enter_context(tc.psum_pool(name="acc", bufs=1))
+
+        raw = {}
+        for j in range(LOAD_BUFS):
+            raw[j] = load_round(nc, raw_pool, input1, input2, W1, j)
+
+        eps = const.tile([P, 1], F32)
+        nc.vector.memset(eps[:], EPS)
+        table_warmer = const.tile([P, 1], F32)
+        ident = const.tile([P, P], F32)
+        make_identity(nc, ident[:])
+
+        bias_rows = const.tile([P, FEATURES], BF16)
+        nc.vector.memset(bias_rows[:], 0.0)
+        ones = const.tile([P, P], BF16)
+        nc.vector.memset(ones[:], 1.0)
+        nc.scalar.dma_start(out=bias_rows[0:1, :], in_=b1.rearrange("(o f) -> o f", o=1))
+        nc.scalar.activation(out=table_warmer[:], in_=eps[:], func=ACT.Sqrt)
+        bias_bank = bank_pool.tile([P, BANK], F32, tag="bank")
+        nc.tensor.matmul(bias_bank[:, 0:FEATURES], lhsT=ones[:], rhs=bias_rows[:], start=True, stop=True)
+        bias = const.tile([P, FEATURES], F32)
+        nc.vector.tensor_copy(out=bias[:], in_=bias_bank[:, 0:FEATURES])
+
+        acc = [acc_pool.tile([P, FEATURES], F32, name="acc%d" % h) for h in range(ROW_BLOCKS)]
+
+        def multiply_round(j, x_codes, x_scales, w_codes, w_scales):
+            for c in range(PASSES_ROUND):
+                w_cols = slice(c * FEATURES, (c + 1) * FEATURES)
+                for h in range(ROW_BLOCKS):
+                    x_cols = slice((c * ROW_BLOCKS + h) * P, (c * ROW_BLOCKS + h + 1) * P)
+                    nc.tensor.matmul_mx(
+                        out=acc[h][:],
+                        lhsT=x_codes[:, x_cols].bitcast(FP8X4),
+                        lhsT_scale=x_scales[:, x_cols],
+                        rhs=w_codes[:, w_cols].bitcast(FP8X4),
+                        rhs_scale=w_scales[:, w_cols],
+                        start=(j == 0 and c == 0),
+                        stop=(j == ROUNDS - 1 and c == PASSES_ROUND - 1),
+                    )
+
+        quantised = {}
+        for j in range(ROUNDS):
+            x_raw, w_raw = raw[j]
+            x_pairs = x_raw[:].bitcast(F32)
+            w_pairs = w_raw[:].bitcast(F32)
+            x_grouped = grouped_pool.tile([P, PASSES_ROUND * ROW_BLOCKS * P * 4], BF16, align_bytes=64)
+            w_grouped = grouped_pool.tile([P, PASSES_ROUND * FEATURES * 4], BF16, align_bytes=64)
+            x_codes = mx_pool.tile([P, PASSES_ROUND * ROW_BLOCKS * P], U32, align_bytes=64)
+            x_scales = mx_pool.tile([P, PASSES_ROUND * ROW_BLOCKS * P], U8, align_bytes=64)
+            w_codes = mx_pool.tile([P, PASSES_ROUND * FEATURES], U32, align_bytes=64)
+            w_scales = mx_pool.tile([P, PASSES_ROUND * FEATURES], U8, align_bytes=64)
+
+            for half in range(2):
+                for c in (2 * half, 2 * half + 1):
+                    starts = [
+                        h * PAIRS_ROUND + c * PAIRS_PASS + u * P for h in range(ROW_BLOCKS) for u in range(2)
+                    ]
+                    bank = transpose_bank(nc, bank_pool, x_pairs, starts, ident)
+                    nc.scalar.copy(out=words_by_row(x_grouped, c), in_=bank_by_row(bank))
+                starts = [half * BANK + s * P for s in range(4)]
+                bank = transpose_bank(nc, bank_pool, w_pairs, starts, ident)
+                nc.vector.tensor_copy(out=words_by_row(w_grouped, half), in_=bank_by_row(bank))
+                if half == 1:
+                    quantise_half(nc, w_grouped, w_codes, w_scales, 0)
+                quantise_half(nc, x_grouped, x_codes, x_scales, half)
+            quantise_half(nc, w_grouped, w_codes, w_scales, 1)
+            quantised[j] = (x_codes, x_scales, w_codes, w_scales)
+
+            if j + LOAD_BUFS < ROUNDS:
+                raw[j + LOAD_BUFS] = load_round(nc, raw_pool, input1, input2, W1, j + LOAD_BUFS)
+            if j >= 1:
+                multiply_round(j - 1, *quantised[j - 1])
+        multiply_round(ROUNDS - 1, *quantised[ROUNDS - 1])
+
+        h_sb = tail.tile([P, ROW_BLOCKS, FEATURES], F32)
+        stats = tail.tile([P, ROW_BLOCKS, 6], F32)
+        mean_var = tail.tile([P, ROW_BLOCKS, 2], F32)
+        std = tail.tile([P, ROW_BLOCKS], F32)
+        rstd = tail.tile([P, ROW_BLOCKS], F32)
+        centred = tail.tile([P, ROW_BLOCKS, FEATURES], F32)
+        leaky = tail.tile([P, ROW_BLOCKS, FEATURES], F32)
+        result = tail.tile([P, ROW_BLOCKS, FEATURES], F32)
+        for h in range(ROW_BLOCKS):
+            nc.vector.tensor_tensor(out=h_sb[:, h, :], in0=acc[h][:], in1=bias[:], op=ALU.add)
+            nc.vector.bn_stats(out=stats[:, h, :], in_=h_sb[:, h, :])
+            nc.vector.bn_aggr(out=mean_var[:, h, :], in_=stats[:, h, :])
+        nc.scalar.activation(out=std[:], in_=mean_var[:, :, 1], func=ACT.Sqrt, bias=eps[:], scale=1.0)
+        for h in range(ROW_BLOCKS):
+            nc.vector.tensor_scalar_sub(out=centred[:, h, :], in0=h_sb[:, h, :], scalar1=mean_var[:, h, 0:1])
+            nc.vector.scalar_tensor_tensor(
+                out=leaky[:, h, :], in0=centred[:, h, :], scalar=SLOPE, in1=centred[:, h, :],
+                op0=ALU.mult, op1=ALU.max,
+            )
+        nc.vector.reciprocal(out=rstd[:], in_=std[:])
+        for h in range(ROW_BLOCKS):
+            nc.vector.tensor_scalar_mul(out=result[:, h, :], in0=leaky[:, h, :], scalar1=rstd[:, h : h + 1])
+        nc.sync.dma_start(out=out.rearrange("(h p) o f -> p h (o f)", p=P), in_=result[:])

@@ -15,58 +15,44 @@ P = 128
 ROW_BLOCKS = 2
 FEATURES = 128
 K_INPUT = 20480
-K_PASS = 512
+PACK = 4
+K_PASS = P * PACK
 PAIRS_PASS = K_PASS // 2
-PASSES_ROUND = 4
-K_ROUND = PASSES_ROUND * K_PASS
-PAIRS_ROUND = K_ROUND // 2
-ROUNDS_INPUT = K_INPUT // K_ROUND
-ROUNDS = 2 * ROUNDS_INPUT
+STEP_PASSES = 2
+K_STEP = STEP_PASSES * K_PASS
+PAIRS_STEP = K_STEP // 2
+STEPS = 2 * K_INPUT // K_STEP
+K_CHUNK = 4096
+CHUNK_STEPS = K_CHUNK // K_STEP
+CHUNKS_INPUT = K_INPUT // K_CHUNK
+CHUNKS = 2 * CHUNKS_INPUT
+RAW_BUFS = 5
 BANK = 512
-LOAD_BUFS = 8
+TRANSPOSE_BANKS = 6
+VECTOR_EVERY = 4
+BUNCH_STEPS = 2
 EPS = 1e-5
 SLOPE = 0.2
 
 FLOPS = 2 * ROW_BLOCKS * P * FEATURES * 2 * K_INPUT
 
 
-def load_round(nc, raw_pool, input1, input2, W1, j):
-    source = input1 if j < ROUNDS_INPUT else input2
-    k0 = (j % ROUNDS_INPUT) * K_ROUND
-    x_raw = raw_pool.tile([P, ROW_BLOCKS * K_ROUND], BF16, tag="x_raw")
-    w_raw = raw_pool.tile([P, K_ROUND], BF16, tag="w_raw")
-    nc.sync.dma_start(
-        out=x_raw[:].rearrange("p (h k) -> p h k", h=ROW_BLOCKS),
-        in_=source.rearrange("(h p) o k -> p h (o k)", p=P)[:, :, k0 : k0 + K_ROUND],
-    )
-    nc.sync.dma_start(out=w_raw[:], in_=W1[:, j * K_ROUND : (j + 1) * K_ROUND])
+def load_chunk(nc, raw_pool, input1, input2, W1, t):
+    source = input1 if t < CHUNKS_INPUT else input2
+    x_rows = source.rearrange("(h p) o k -> p h (o k)", p=P)
+    k0 = (t % CHUNKS_INPUT) * K_CHUNK
+    x_raw = raw_pool.tile([P, ROW_BLOCKS * K_CHUNK], BF16, tag="x_raw")
+    w_raw = raw_pool.tile([P, K_CHUNK], BF16, tag="w_raw")
+    x_view = x_raw[:].rearrange("p (h k) -> p h k", h=ROW_BLOCKS)
+    width = K_STEP if t in (0, CHUNKS - 1) else K_CHUNK
+    for a in range(0, K_CHUNK, width):
+        nc.sync.dma_start(out=x_view[:, :, a : a + width], in_=x_rows[:, :, k0 + a : k0 + a + width])
+        nc.sync.dma_start(out=w_raw[:, a : a + width], in_=W1[:, t * K_CHUNK + a : t * K_CHUNK + a + width])
     return x_raw, w_raw
 
 
-def transpose_bank(nc, bank_pool, pairs, starts, ident):
-    bank = bank_pool.tile([P, BANK], F32, tag="bank")
-    for s, start in enumerate(starts):
-        nc.tensor.transpose(bank[:, s * P : (s + 1) * P], pairs[:, start : start + P], ident[:])
-    return bank
-
-
-def bank_by_row(bank):
-    return bank[:].rearrange("p (n u r) -> p n r u", n=2, u=2)
-
-
-def words_by_row(grouped, first_bank):
-    pairs = grouped[:].bitcast(F32)[:, first_bank * BANK : (first_bank + 1) * BANK]
-    return pairs.rearrange("p (n r u) -> p n r u", n=2, u=2)
-
-
-def quantise_half(nc, grouped, codes, scales, half):
-    width = codes.shape[1] // 2
-    cols = slice(half * width, (half + 1) * width)
-    nc.vector.quantize_mx(
-        out=codes[:, cols].bitcast(FP8X4),
-        scales=scales[:, cols],
-        in_=grouped[:, half * width * 4 : (half + 1) * width * 4],
-    )
+def quantise(nc, grouped, codes, scales):
+    nc.vector.quantize_mx(out=codes[:].bitcast(FP8X4), scales=scales[:], in_=grouped[:])
 
 
 def tile_fcd_pa_kernel(tc, input1, input2, W1, b1, out):
@@ -74,38 +60,80 @@ def tile_fcd_pa_kernel(tc, input1, input2, W1, b1, out):
     with ExitStack() as ctx:
         ctx.enter_context(tc.manual_schedule())
         const = ctx.enter_context(tc.tile_pool(name="const", bufs=1))
-        raw_pool = ctx.enter_context(tc.tile_pool(name="raw", bufs=LOAD_BUFS))
-        grouped_pool = ctx.enter_context(tc.tile_pool(name="grouped", bufs=2))
-        mx_pool = ctx.enter_context(tc.tile_pool(name="mx", bufs=3))
+        raw_pool = ctx.enter_context(tc.tile_pool(name="raw", bufs=RAW_BUFS))
+        grouped_pool = ctx.enter_context(tc.tile_pool(name="grouped", bufs=3))
+        mx_pool = ctx.enter_context(tc.tile_pool(name="mx", bufs=6))
         tail = ctx.enter_context(tc.tile_pool(name="tail", bufs=1))
-        bank_pool = ctx.enter_context(tc.psum_pool(name="banks", bufs=6))
+        bank_pool = ctx.enter_context(tc.psum_pool(name="banks", bufs=TRANSPOSE_BANKS))
         acc_pool = ctx.enter_context(tc.psum_pool(name="acc", bufs=1))
-
-        raw = {}
-        for j in range(LOAD_BUFS):
-            raw[j] = load_round(nc, raw_pool, input1, input2, W1, j)
-
-        eps = const.tile([P, 1], F32)
-        nc.vector.memset(eps[:], EPS)
-        table_warmer = const.tile([P, 1], F32)
-        ident = const.tile([P, P], F32)
-        make_identity(nc, ident[:])
 
         bias_rows = const.tile([P, FEATURES], BF16)
         nc.vector.memset(bias_rows[:], 0.0)
+        nc.scalar.dma_start(out=bias_rows[0:1, :], in_=b1.rearrange("(o f) -> o f", o=1))
+
+        raw = {}
+        for t in range(RAW_BUFS):
+            raw[t] = load_chunk(nc, raw_pool, input1, input2, W1, t)
+
+        one = const.tile([P, 1], F32)
+        nc.vector.memset(one[:], 1.0)
+        table_warmer = const.tile([P, 1], F32)
+        nc.scalar.activation(out=table_warmer[:], in_=one[:], func=ACT.Sqrt)
+        ident = const.tile([P, P], F32)
+        make_identity(nc, ident[:])
+
         ones = const.tile([P, P], BF16)
         nc.vector.memset(ones[:], 1.0)
-        nc.scalar.dma_start(out=bias_rows[0:1, :], in_=b1.rearrange("(o f) -> o f", o=1))
-        nc.scalar.activation(out=table_warmer[:], in_=eps[:], func=ACT.Sqrt)
         bias_bank = bank_pool.tile([P, BANK], F32, tag="bank")
         nc.tensor.matmul(bias_bank[:, 0:FEATURES], lhsT=ones[:], rhs=bias_rows[:], start=True, stop=True)
         bias = const.tile([P, FEATURES], F32)
         nc.vector.tensor_copy(out=bias[:], in_=bias_bank[:, 0:FEATURES])
 
         acc = [acc_pool.tile([P, FEATURES], F32, name="acc%d" % h) for h in range(ROW_BLOCKS)]
+        grouped = {}
+        quantised = {}
 
-        def multiply_round(j, x_codes, x_scales, w_codes, w_scales):
-            for c in range(PASSES_ROUND):
+        def transpose_bank(n, pairs, starts, target):
+            bank = bank_pool.tile([P, BANK], F32, tag="bank")
+            for s, start in enumerate(starts):
+                nc.tensor.transpose(bank[:, s * P : (s + 1) * P], pairs[:, start : start + P], ident[:])
+            by_row = bank[:].rearrange("p (n u r) -> p n r u", n=2, u=2)
+            target_by_row = target.bitcast(F32).rearrange("p (n r u) -> p n r u", n=2, u=2)
+            if n % VECTOR_EVERY == VECTOR_EVERY - 1:
+                nc.vector.tensor_copy(out=target_by_row, in_=by_row)
+            else:
+                nc.scalar.copy(out=target_by_row, in_=by_row)
+
+        def transpose_step(i):
+            x_raw, w_raw = raw[i // CHUNK_STEPS]
+            first = (i % CHUNK_STEPS) * PAIRS_STEP
+            x_grouped = grouped_pool.tile([P, STEP_PASSES * ROW_BLOCKS * P * PACK], BF16, align_bytes=64)
+            w_grouped = grouped_pool.tile([P, STEP_PASSES * FEATURES * PACK], BF16, align_bytes=64)
+            for c in range(STEP_PASSES):
+                starts = [
+                    h * (K_CHUNK // 2) + first + c * PAIRS_PASS + u * P
+                    for h in range(ROW_BLOCKS)
+                    for u in range(2)
+                ]
+                target = x_grouped[:, c * 2 * BANK : (c + 1) * 2 * BANK]
+                transpose_bank(3 * i + c, x_raw[:].bitcast(F32), starts, target)
+            starts = [first + s * P for s in range(4)]
+            transpose_bank(3 * i + 2, w_raw[:].bitcast(F32), starts, w_grouped[:])
+            grouped[i] = (x_grouped, w_grouped)
+
+        def quantise_step(i):
+            x_grouped, w_grouped = grouped[i]
+            x_codes = mx_pool.tile([P, STEP_PASSES * ROW_BLOCKS * P], U32, align_bytes=64)
+            x_scales = mx_pool.tile([P, STEP_PASSES * ROW_BLOCKS * P], U8, align_bytes=64)
+            w_codes = mx_pool.tile([P, STEP_PASSES * FEATURES], U32, align_bytes=64)
+            w_scales = mx_pool.tile([P, STEP_PASSES * FEATURES], U8, align_bytes=64)
+            quantise(nc, x_grouped, x_codes, x_scales)
+            quantise(nc, w_grouped, w_codes, w_scales)
+            quantised[i] = (x_codes, x_scales, w_codes, w_scales)
+
+        def multiply_step(i):
+            x_codes, x_scales, w_codes, w_scales = quantised[i]
+            for c in range(STEP_PASSES):
                 w_cols = slice(c * FEATURES, (c + 1) * FEATURES)
                 for h in range(ROW_BLOCKS):
                     x_cols = slice((c * ROW_BLOCKS + h) * P, (c * ROW_BLOCKS + h + 1) * P)
@@ -115,43 +143,23 @@ def tile_fcd_pa_kernel(tc, input1, input2, W1, b1, out):
                         lhsT_scale=x_scales[:, x_cols],
                         rhs=w_codes[:, w_cols].bitcast(FP8X4),
                         rhs_scale=w_scales[:, w_cols],
-                        start=(j == 0 and c == 0),
-                        stop=(j == ROUNDS - 1 and c == PASSES_ROUND - 1),
+                        start=(i == 0 and c == 0),
+                        stop=(i == STEPS - 1 and c == STEP_PASSES - 1),
                     )
 
-        quantised = {}
-        for j in range(ROUNDS):
-            x_raw, w_raw = raw[j]
-            x_pairs = x_raw[:].bitcast(F32)
-            w_pairs = w_raw[:].bitcast(F32)
-            x_grouped = grouped_pool.tile([P, PASSES_ROUND * ROW_BLOCKS * P * 4], BF16, align_bytes=64)
-            w_grouped = grouped_pool.tile([P, PASSES_ROUND * FEATURES * 4], BF16, align_bytes=64)
-            x_codes = mx_pool.tile([P, PASSES_ROUND * ROW_BLOCKS * P], U32, align_bytes=64)
-            x_scales = mx_pool.tile([P, PASSES_ROUND * ROW_BLOCKS * P], U8, align_bytes=64)
-            w_codes = mx_pool.tile([P, PASSES_ROUND * FEATURES], U32, align_bytes=64)
-            w_scales = mx_pool.tile([P, PASSES_ROUND * FEATURES], U8, align_bytes=64)
-
-            for half in range(2):
-                for c in (2 * half, 2 * half + 1):
-                    starts = [
-                        h * PAIRS_ROUND + c * PAIRS_PASS + u * P for h in range(ROW_BLOCKS) for u in range(2)
-                    ]
-                    bank = transpose_bank(nc, bank_pool, x_pairs, starts, ident)
-                    nc.scalar.copy(out=words_by_row(x_grouped, c), in_=bank_by_row(bank))
-                starts = [half * BANK + s * P for s in range(4)]
-                bank = transpose_bank(nc, bank_pool, w_pairs, starts, ident)
-                nc.vector.tensor_copy(out=words_by_row(w_grouped, half), in_=bank_by_row(bank))
-                if half == 1:
-                    quantise_half(nc, w_grouped, w_codes, w_scales, 0)
-                quantise_half(nc, x_grouped, x_codes, x_scales, half)
-            quantise_half(nc, w_grouped, w_codes, w_scales, 1)
-            quantised[j] = (x_codes, x_scales, w_codes, w_scales)
-
-            if j + LOAD_BUFS < ROUNDS:
-                raw[j + LOAD_BUFS] = load_round(nc, raw_pool, input1, input2, W1, j + LOAD_BUFS)
-            if j >= 1:
-                multiply_round(j - 1, *quantised[j - 1])
-        multiply_round(ROUNDS - 1, *quantised[ROUNDS - 1])
+        for i in range(STEPS):
+            transpose_step(i)
+            if i % CHUNK_STEPS == CHUNK_STEPS - 1 and i // CHUNK_STEPS + RAW_BUFS < CHUNKS:
+                t = i // CHUNK_STEPS + RAW_BUFS
+                raw[t] = load_chunk(nc, raw_pool, input1, input2, W1, t)
+            if i >= 1:
+                quantise_step(i - 1)
+            if i > BUNCH_STEPS and i % BUNCH_STEPS == BUNCH_STEPS - 1:
+                for done in range(i - 2 * BUNCH_STEPS + 1, i - BUNCH_STEPS + 1):
+                    multiply_step(done)
+        quantise_step(STEPS - 1)
+        for done in range(STEPS - BUNCH_STEPS, STEPS):
+            multiply_step(done)
 
         h_sb = tail.tile([P, ROW_BLOCKS, FEATURES], F32)
         stats = tail.tile([P, ROW_BLOCKS, 6], F32)
@@ -165,12 +173,16 @@ def tile_fcd_pa_kernel(tc, input1, input2, W1, b1, out):
             nc.vector.tensor_tensor(out=h_sb[:, h, :], in0=acc[h][:], in1=bias[:], op=ALU.add)
             nc.vector.bn_stats(out=stats[:, h, :], in_=h_sb[:, h, :])
             nc.vector.bn_aggr(out=mean_var[:, h, :], in_=stats[:, h, :])
-        nc.scalar.activation(out=std[:], in_=mean_var[:, :, 1], func=ACT.Sqrt, bias=eps[:], scale=1.0)
+        nc.scalar.activation(out=std[:], in_=mean_var[:, :, 1], func=ACT.Sqrt, bias=EPS, scale=1.0)
         for h in range(ROW_BLOCKS):
             nc.vector.tensor_scalar_sub(out=centred[:, h, :], in0=h_sb[:, h, :], scalar1=mean_var[:, h, 0:1])
             nc.vector.scalar_tensor_tensor(
-                out=leaky[:, h, :], in0=centred[:, h, :], scalar=SLOPE, in1=centred[:, h, :],
-                op0=ALU.mult, op1=ALU.max,
+                out=leaky[:, h, :],
+                in0=centred[:, h, :],
+                scalar=SLOPE,
+                in1=centred[:, h, :],
+                op0=ALU.mult,
+                op1=ALU.max,
             )
         nc.vector.reciprocal(out=rstd[:], in_=std[:])
         for h in range(ROW_BLOCKS):

@@ -12,57 +12,46 @@ ALU = mybir.AluOpType
 ACT = mybir.ActivationFunctionType
 
 P = 128
-ROW_BLOCKS = 2
+X_BLOCKS = 2
+BLOCKS = X_BLOCKS + 1
+W_BLOCK = X_BLOCKS
 FEATURES = 128
 K_INPUT = 20480
 PACK = 4
 K_PASS = P * PACK
-PAIRS_PASS = K_PASS // 2
-STEP_PASSES = 2
-K_STEP = STEP_PASSES * K_PASS
-PAIRS_STEP = K_STEP // 2
-STEPS = 2 * K_INPUT // K_STEP
-K_CHUNK = 4096
-CHUNK_STEPS = K_CHUNK // K_STEP
-CHUNKS_INPUT = K_INPUT // K_CHUNK
-CHUNKS = 2 * CHUNKS_INPUT
-RAW_BUFS = 5
 BANK = 512
+K_BANK = 2 * BANK
+BANK_PASSES = K_BANK // K_PASS
+UNIT_BANKS = 2
+UNIT_PASSES = UNIT_BANKS * BANK_PASSES
+K_CHUNK = 4096
+CHUNK_PASSES = K_CHUNK // K_PASS
+CHUNKS = 2 * K_INPUT // K_CHUNK
+TAPER_CHUNKS = 2
+RAW_BUFS = 12
 TRANSPOSE_BANKS = 6
 VECTOR_EVERY = 4
-BUNCH_STEPS = 2
+RUN_BANKS = 6
 EPS = 1e-5
 SLOPE = 0.2
 
-FLOPS = 2 * ROW_BLOCKS * P * FEATURES * 2 * K_INPUT
+FLOPS = 2 * X_BLOCKS * P * FEATURES * 2 * K_INPUT
 
 
-def load_chunk(nc, raw_pool, input1, input2, W1, t):
-    source = input1 if t < CHUNKS_INPUT else input2
-    x_rows = source.rearrange("(h p) o k -> p h (o k)", p=P)
-    k0 = (t % CHUNKS_INPUT) * K_CHUNK
-    x_raw = raw_pool.tile([P, ROW_BLOCKS * K_CHUNK], BF16, tag="x_raw")
-    w_raw = raw_pool.tile([P, K_CHUNK], BF16, tag="w_raw")
-    x_view = x_raw[:].rearrange("p (h k) -> p h k", h=ROW_BLOCKS)
-    width = K_STEP if t in (0, CHUNKS - 1) else K_CHUNK
-    for a in range(0, K_CHUNK, width):
-        nc.sync.dma_start(out=x_view[:, :, a : a + width], in_=x_rows[:, :, k0 + a : k0 + a + width])
-        nc.sync.dma_start(out=w_raw[:, a : a + width], in_=W1[:, t * K_CHUNK + a : t * K_CHUNK + a + width])
-    return x_raw, w_raw
-
-
-def quantise(nc, grouped, codes, scales):
-    nc.vector.quantize_mx(out=codes[:].bitcast(FP8X4), scales=scales[:], in_=grouped[:])
+def chunk_list():
+    widths = [K_CHUNK] * (CHUNKS - TAPER_CHUNKS) + [K_CHUNK // 2] * (2 * TAPER_CHUNKS)
+    return [(sum(widths[:j]), width) for j, width in enumerate(widths)]
 
 
 def tile_fcd_pa_kernel(tc, input1, input2, W1, b1, out):
     nc = tc.nc
+    chunks = chunk_list()
     with ExitStack() as ctx:
         ctx.enter_context(tc.manual_schedule())
         const = ctx.enter_context(tc.tile_pool(name="const", bufs=1))
         raw_pool = ctx.enter_context(tc.tile_pool(name="raw", bufs=RAW_BUFS))
-        grouped_pool = ctx.enter_context(tc.tile_pool(name="grouped", bufs=3))
-        mx_pool = ctx.enter_context(tc.tile_pool(name="mx", bufs=6))
+        grouped_pool = ctx.enter_context(tc.tile_pool(name="grouped", bufs=4))
+        mx_pool = ctx.enter_context(tc.tile_pool(name="mx", bufs=3))
         tail = ctx.enter_context(tc.tile_pool(name="tail", bufs=1))
         bank_pool = ctx.enter_context(tc.psum_pool(name="banks", bufs=TRANSPOSE_BANKS))
         acc_pool = ctx.enter_context(tc.psum_pool(name="acc", bufs=1))
@@ -72,8 +61,21 @@ def tile_fcd_pa_kernel(tc, input1, input2, W1, b1, out):
         nc.scalar.dma_start(out=bias_rows[0:1, :], in_=b1.rearrange("(o f) -> o f", o=1))
 
         raw = {}
-        for t in range(RAW_BUFS):
-            raw[t] = load_chunk(nc, raw_pool, input1, input2, W1, t)
+
+        def load(m):
+            k0, width = chunks[m // BLOCKS]
+            block = m % BLOCKS
+            if block == W_BLOCK:
+                rows = W1[:, k0 : k0 + width]
+            else:
+                source = input1 if k0 < K_INPUT else input2
+                first = k0 % K_INPUT
+                rows = source.rearrange("b o k -> b (o k)")[block * P : (block + 1) * P, first : first + width]
+            raw[m] = raw_pool.tile([P, K_CHUNK], BF16, name="raw_tile")
+            nc.sync.dma_start(out=raw[m][:, 0:width], in_=rows)
+
+        for m in range(RAW_BUFS):
+            load(m)
 
         one = const.tile([P, 1], F32)
         nc.vector.memset(one[:], 1.0)
@@ -89,93 +91,93 @@ def tile_fcd_pa_kernel(tc, input1, input2, W1, b1, out):
         bias = const.tile([P, FEATURES], F32)
         nc.vector.tensor_copy(out=bias[:], in_=bias_bank[:, 0:FEATURES])
 
-        acc = [acc_pool.tile([P, FEATURES], F32, name="acc%d" % h) for h in range(ROW_BLOCKS)]
-        grouped = {}
-        quantised = {}
+        acc = [acc_pool.tile([P, FEATURES], F32, name="acc%d" % h) for h in range(X_BLOCKS)]
 
-        def transpose_bank(n, pairs, starts, target):
+        def transpose_bank(n, pairs, target):
             bank = bank_pool.tile([P, BANK], F32, tag="bank")
-            for s, start in enumerate(starts):
-                nc.tensor.transpose(bank[:, s * P : (s + 1) * P], pairs[:, start : start + P], ident[:])
-            by_row = bank[:].rearrange("p (n u r) -> p n r u", n=2, u=2)
-            target_by_row = target.bitcast(F32).rearrange("p (n r u) -> p n r u", n=2, u=2)
-            if n % VECTOR_EVERY == VECTOR_EVERY - 1:
+            for s in range(BANK // P):
+                nc.tensor.transpose(bank[:, s * P : (s + 1) * P], pairs[:, s * P : (s + 1) * P], ident[:])
+            by_row = bank[:].rearrange("p (c u r) -> p c r u", c=BANK_PASSES, u=2)
+            target_by_row = target.bitcast(F32).rearrange("p (c r u) -> p c r u", c=BANK_PASSES, u=2)
+            if n % VECTOR_EVERY == 0:
                 nc.vector.tensor_copy(out=target_by_row, in_=by_row)
             else:
                 nc.scalar.copy(out=target_by_row, in_=by_row)
 
-        def transpose_step(i):
-            x_raw, w_raw = raw[i // CHUNK_STEPS]
-            first = (i % CHUNK_STEPS) * PAIRS_STEP
-            x_grouped = grouped_pool.tile([P, STEP_PASSES * ROW_BLOCKS * P * PACK], BF16, align_bytes=64)
-            w_grouped = grouped_pool.tile([P, STEP_PASSES * FEATURES * PACK], BF16, align_bytes=64)
-            for c in range(STEP_PASSES):
-                starts = [
-                    h * (K_CHUNK // 2) + first + c * PAIRS_PASS + u * P
-                    for h in range(ROW_BLOCKS)
-                    for u in range(2)
-                ]
-                target = x_grouped[:, c * 2 * BANK : (c + 1) * 2 * BANK]
-                transpose_bank(3 * i + c, x_raw[:].bitcast(F32), starts, target)
-            starts = [first + s * P for s in range(4)]
-            transpose_bank(3 * i + 2, w_raw[:].bitcast(F32), starts, w_grouped[:])
-            grouped[i] = (x_grouped, w_grouped)
+        def quantise(grouped, codes, scales, first_word):
+            words = slice(first_word, first_word + UNIT_PASSES * P)
+            nc.vector.quantize_mx(out=codes[:, words].bitcast(FP8X4), scales=scales[:, words], in_=grouped[:])
 
-        def quantise_step(i):
-            x_grouped, w_grouped = grouped[i]
-            x_codes = mx_pool.tile([P, STEP_PASSES * ROW_BLOCKS * P], U32, align_bytes=64)
-            x_scales = mx_pool.tile([P, STEP_PASSES * ROW_BLOCKS * P], U8, align_bytes=64)
-            w_codes = mx_pool.tile([P, STEP_PASSES * FEATURES], U32, align_bytes=64)
-            w_scales = mx_pool.tile([P, STEP_PASSES * FEATURES], U8, align_bytes=64)
-            quantise(nc, x_grouped, x_codes, x_scales)
-            quantise(nc, w_grouped, w_codes, w_scales)
-            quantised[i] = (x_codes, x_scales, w_codes, w_scales)
-
-        def multiply_step(i):
-            x_codes, x_scales, w_codes, w_scales = quantised[i]
-            for c in range(STEP_PASSES):
-                w_cols = slice(c * FEATURES, (c + 1) * FEATURES)
-                for h in range(ROW_BLOCKS):
-                    x_cols = slice((c * ROW_BLOCKS + h) * P, (c * ROW_BLOCKS + h + 1) * P)
+        def multiply(j, passes):
+            codes, scales = packed[j]
+            last_pass = chunks[j][1] // K_PASS - 1
+            for h in range(X_BLOCKS):
+                for c in passes:
+                    x_words = slice((h * CHUNK_PASSES + c) * P, (h * CHUNK_PASSES + c + 1) * P)
+                    w_words = slice((W_BLOCK * CHUNK_PASSES + c) * P, (W_BLOCK * CHUNK_PASSES + c + 1) * P)
                     nc.tensor.matmul_mx(
                         out=acc[h][:],
-                        lhsT=x_codes[:, x_cols].bitcast(FP8X4),
-                        lhsT_scale=x_scales[:, x_cols],
-                        rhs=w_codes[:, w_cols].bitcast(FP8X4),
-                        rhs_scale=w_scales[:, w_cols],
-                        start=(i == 0 and c == 0),
-                        stop=(i == STEPS - 1 and c == STEP_PASSES - 1),
+                        lhsT=codes[:, x_words].bitcast(FP8X4),
+                        lhsT_scale=scales[:, x_words],
+                        rhs=codes[:, w_words].bitcast(FP8X4),
+                        rhs_scale=scales[:, w_words],
+                        start=(j == 0 and c == 0),
+                        stop=(j == len(chunks) - 1 and c == last_pass),
                     )
 
-        for i in range(STEPS):
-            transpose_step(i)
-            if i % CHUNK_STEPS == CHUNK_STEPS - 1 and i // CHUNK_STEPS + RAW_BUFS < CHUNKS:
-                t = i // CHUNK_STEPS + RAW_BUFS
-                raw[t] = load_chunk(nc, raw_pool, input1, input2, W1, t)
-            if i >= 1:
-                quantise_step(i - 1)
-            if i > BUNCH_STEPS and i % BUNCH_STEPS == BUNCH_STEPS - 1:
-                for done in range(i - 2 * BUNCH_STEPS + 1, i - BUNCH_STEPS + 1):
-                    multiply_step(done)
-        quantise_step(STEPS - 1)
-        for done in range(STEPS - BUNCH_STEPS, STEPS):
-            multiply_step(done)
+        packed = {}
+        waiting = None
+        n = 0
+        for j in range(len(chunks)):
+            codes = mx_pool.tile([P, BLOCKS * CHUNK_PASSES * P], U32, align_bytes=64)
+            scales = mx_pool.tile([P, BLOCKS * CHUNK_PASSES * P], U8, align_bytes=64)
+            packed[j] = (codes, scales)
+            chunk_banks = chunks[j][1] // K_BANK
+            runs = BLOCKS * chunk_banks // RUN_BANKS
+            share = chunks[j - 1][1] // K_PASS // runs if j > 0 else 0
+            for block in range(BLOCKS):
+                m = j * BLOCKS + block
+                pairs = raw[m][:].bitcast(F32)
+                for b in range(chunk_banks):
+                    half = b % UNIT_BANKS
+                    if half == 0:
+                        grouped = grouped_pool.tile([P, UNIT_BANKS * 2 * BANK], BF16, align_bytes=64)
+                    transpose_bank(
+                        n, pairs[:, b * BANK : (b + 1) * BANK], grouped[:, half * 2 * BANK : (half + 1) * 2 * BANK]
+                    )
+                    n += 1
+                    if half == UNIT_BANKS - 1:
+                        if waiting is not None:
+                            quantise(*waiting)
+                        first_word = (block * CHUNK_PASSES + (b - half) * BANK_PASSES) * P
+                        waiting = (grouped, codes, scales, first_word)
+                    done = block * chunk_banks + b + 1
+                    if j > 0 and done % RUN_BANKS == 0:
+                        run = done // RUN_BANKS
+                        multiply(j - 1, range((run - 1) * share, run * share))
+                if m + RAW_BUFS < BLOCKS * len(chunks):
+                    load(m + RAW_BUFS)
+        quantise(*waiting)
+        multiply(len(chunks) - 1, range(chunks[-1][1] // K_PASS))
 
-        h_sb = tail.tile([P, ROW_BLOCKS, FEATURES], F32)
-        stats = tail.tile([P, ROW_BLOCKS, 6], F32)
-        mean_var = tail.tile([P, ROW_BLOCKS, 2], F32)
-        std = tail.tile([P, ROW_BLOCKS], F32)
-        rstd = tail.tile([P, ROW_BLOCKS], F32)
-        centred = tail.tile([P, ROW_BLOCKS, FEATURES], F32)
-        leaky = tail.tile([P, ROW_BLOCKS, FEATURES], F32)
-        result = tail.tile([P, ROW_BLOCKS, FEATURES], F32)
-        for h in range(ROW_BLOCKS):
+        h_sb = tail.tile([P, X_BLOCKS, FEATURES], F32)
+        stats = tail.tile([P, X_BLOCKS, 6], F32)
+        mean_var = tail.tile([P, X_BLOCKS, 2], F32)
+        std = tail.tile([P, X_BLOCKS], F32)
+        rstd = tail.tile([P, X_BLOCKS], F32)
+        centred = tail.tile([P, X_BLOCKS, FEATURES], F32)
+        leaky = tail.tile([P, X_BLOCKS, FEATURES], F32)
+        result = tail.tile([P, X_BLOCKS, FEATURES], F32)
+        for h in range(X_BLOCKS):
             nc.vector.tensor_tensor(out=h_sb[:, h, :], in0=acc[h][:], in1=bias[:], op=ALU.add)
+        for h in range(X_BLOCKS):
             nc.vector.bn_stats(out=stats[:, h, :], in_=h_sb[:, h, :])
+        for h in range(X_BLOCKS):
             nc.vector.bn_aggr(out=mean_var[:, h, :], in_=stats[:, h, :])
         nc.scalar.activation(out=std[:], in_=mean_var[:, :, 1], func=ACT.Sqrt, bias=EPS, scale=1.0)
-        for h in range(ROW_BLOCKS):
+        for h in range(X_BLOCKS):
             nc.vector.tensor_scalar_sub(out=centred[:, h, :], in0=h_sb[:, h, :], scalar1=mean_var[:, h, 0:1])
+        for h in range(X_BLOCKS):
             nc.vector.scalar_tensor_tensor(
                 out=leaky[:, h, :],
                 in0=centred[:, h, :],
@@ -185,6 +187,6 @@ def tile_fcd_pa_kernel(tc, input1, input2, W1, b1, out):
                 op1=ALU.max,
             )
         nc.vector.reciprocal(out=rstd[:], in_=std[:])
-        for h in range(ROW_BLOCKS):
+        for h in range(X_BLOCKS):
             nc.vector.tensor_scalar_mul(out=result[:, h, :], in0=leaky[:, h, :], scalar1=rstd[:, h : h + 1])
         nc.sync.dma_start(out=out.rearrange("(h p) o f -> p h (o f)", p=P), in_=result[:])

@@ -14,7 +14,8 @@ ACT = mybir.ActivationFunctionType
 P = 128
 X_BLOCKS = 2
 BLOCKS = X_BLOCKS + 1
-W_BLOCK = X_BLOCKS
+W_BLOCK = 0
+X_FIRST = 1
 FEATURES = 128
 K_INPUT = 20480
 PACK = 4
@@ -70,7 +71,8 @@ def tile_fcd_pa_kernel(tc, input1, input2, W1, b1, out):
             else:
                 source = input1 if k0 < K_INPUT else input2
                 first = k0 % K_INPUT
-                rows = source.rearrange("b o k -> b (o k)")[block * P : (block + 1) * P, first : first + width]
+                h = block - X_FIRST
+                rows = source.rearrange("b o k -> b (o k)")[h * P : (h + 1) * P, first : first + width]
             raw[m] = raw_pool.tile([P, K_CHUNK], BF16, name="raw_tile")
             nc.sync.dma_start(out=raw[m][:, 0:width], in_=rows)
 
@@ -80,7 +82,7 @@ def tile_fcd_pa_kernel(tc, input1, input2, W1, b1, out):
         one = const.tile([P, 1], F32)
         nc.vector.memset(one[:], 1.0)
         table_warmer = const.tile([P, 1], F32)
-        nc.scalar.activation(out=table_warmer[:], in_=one[:], func=ACT.Sqrt)
+        nc.scalar.activation(out=table_warmer[:], in_=one[:], func=ACT.Abs_reciprocal_sqrt)
         ident = const.tile([P, P], F32)
         make_identity(nc, ident[:])
 
@@ -108,12 +110,13 @@ def tile_fcd_pa_kernel(tc, input1, input2, W1, b1, out):
             words = slice(first_word, first_word + UNIT_PASSES * P)
             nc.vector.quantize_mx(out=codes[:, words].bitcast(FP8X4), scales=scales[:, words], in_=grouped[:])
 
-        def multiply(j, passes):
+        def multiply(j, passes, halves=range(X_BLOCKS)):
             codes, scales = packed[j]
             last_pass = chunks[j][1] // K_PASS - 1
-            for h in range(X_BLOCKS):
+            for h in halves:
                 for c in passes:
-                    x_words = slice((h * CHUNK_PASSES + c) * P, (h * CHUNK_PASSES + c + 1) * P)
+                    x_slot = (X_FIRST + h) * CHUNK_PASSES + c
+                    x_words = slice(x_slot * P, (x_slot + 1) * P)
                     w_words = slice((W_BLOCK * CHUNK_PASSES + c) * P, (W_BLOCK * CHUNK_PASSES + c + 1) * P)
                     nc.tensor.matmul_mx(
                         out=acc[h][:],
@@ -128,6 +131,7 @@ def tile_fcd_pa_kernel(tc, input1, input2, W1, b1, out):
         packed = {}
         waiting = None
         n = 0
+        last = len(chunks) - 1
         for j in range(len(chunks)):
             codes = mx_pool.tile([P, BLOCKS * CHUNK_PASSES * P], U32, align_bytes=64)
             scales = mx_pool.tile([P, BLOCKS * CHUNK_PASSES * P], U8, align_bytes=64)
@@ -138,6 +142,8 @@ def tile_fcd_pa_kernel(tc, input1, input2, W1, b1, out):
             for block in range(BLOCKS):
                 m = j * BLOCKS + block
                 pairs = raw[m][:].bitcast(F32)
+                if j == last and block == BLOCKS - 1:
+                    multiply(j - 1, range(chunks[j - 1][1] // K_PASS))
                 for b in range(chunk_banks):
                     half = b % UNIT_BANKS
                     if half == 0:
@@ -151,33 +157,42 @@ def tile_fcd_pa_kernel(tc, input1, input2, W1, b1, out):
                             quantise(*waiting)
                         first_word = (block * CHUNK_PASSES + (b - half) * BANK_PASSES) * P
                         waiting = (grouped, codes, scales, first_word)
+                        if j == last:
+                            quantise(*waiting)
+                            waiting = None
                     done = block * chunk_banks + b + 1
-                    if j > 0 and done % RUN_BANKS == 0:
+                    if 0 < j < last and done % RUN_BANKS == 0:
                         run = done // RUN_BANKS
                         multiply(j - 1, range((run - 1) * share, run * share))
                 if m + RAW_BUFS < BLOCKS * len(chunks):
                     load(m + RAW_BUFS)
-        quantise(*waiting)
-        multiply(len(chunks) - 1, range(chunks[-1][1] // K_PASS))
+        for h in range(X_BLOCKS):
+            multiply(last, range(chunks[last][1] // K_PASS), halves=[h])
 
         h_sb = tail.tile([P, X_BLOCKS, FEATURES], F32)
         stats = tail.tile([P, X_BLOCKS, 6], F32)
         mean_var = tail.tile([P, X_BLOCKS, 2], F32)
-        std = tail.tile([P, X_BLOCKS], F32)
-        rstd = tail.tile([P, X_BLOCKS], F32)
         centred = tail.tile([P, X_BLOCKS, FEATURES], F32)
         leaky = tail.tile([P, X_BLOCKS, FEATURES], F32)
-        result = tail.tile([P, X_BLOCKS, FEATURES], F32)
-        for h in range(X_BLOCKS):
+        rstd = [tail.tile([P, 1], F32, name="rstd%d" % h) for h in range(X_BLOCKS)]
+        result = [tail.tile([P, FEATURES], F32, name="result%d" % h) for h in range(X_BLOCKS)]
+
+        def add_bias(h):
             nc.vector.tensor_tensor(out=h_sb[:, h, :], in0=acc[h][:], in1=bias[:], op=ALU.add)
-        for h in range(X_BLOCKS):
+
+        def take_stats(h):
             nc.vector.bn_stats(out=stats[:, h, :], in_=h_sb[:, h, :])
-        for h in range(X_BLOCKS):
+
+        def take_mean_var(h):
             nc.vector.bn_aggr(out=mean_var[:, h, :], in_=stats[:, h, :])
-        nc.scalar.activation(out=std[:], in_=mean_var[:, :, 1], func=ACT.Sqrt, bias=EPS, scale=1.0)
-        for h in range(X_BLOCKS):
+            nc.scalar.activation(
+                out=rstd[h][:], in_=mean_var[:, h, 1:2], func=ACT.Abs_reciprocal_sqrt, bias=EPS, scale=1.0
+            )
+
+        def centre(h):
             nc.vector.tensor_scalar_sub(out=centred[:, h, :], in0=h_sb[:, h, :], scalar1=mean_var[:, h, 0:1])
-        for h in range(X_BLOCKS):
+
+        def relu(h):
             nc.vector.scalar_tensor_tensor(
                 out=leaky[:, h, :],
                 in0=centred[:, h, :],
@@ -186,7 +201,20 @@ def tile_fcd_pa_kernel(tc, input1, input2, W1, b1, out):
                 op0=ALU.mult,
                 op1=ALU.max,
             )
-        nc.vector.reciprocal(out=rstd[:], in_=std[:])
-        for h in range(X_BLOCKS):
-            nc.vector.tensor_scalar_mul(out=result[:, h, :], in0=leaky[:, h, :], scalar1=rstd[:, h : h + 1])
-        nc.sync.dma_start(out=out.rearrange("(h p) o f -> p h (o f)", p=P), in_=result[:])
+
+        def store(h, queue):
+            nc.vector.tensor_scalar_mul(out=result[h][:], in0=leaky[:, h, :], scalar1=rstd[h][:])
+            queue.dma_start(out=out.rearrange("b o f -> b (o f)")[h * P : (h + 1) * P, :], in_=result[h][:])
+
+        add_bias(0)
+        take_stats(0)
+        take_mean_var(0)
+        add_bias(1)
+        centre(0)
+        take_stats(1)
+        relu(0)
+        take_mean_var(1)
+        store(0, nc.scalar)
+        centre(1)
+        relu(1)
+        store(1, nc.sync)

@@ -25,11 +25,11 @@ K_BANK = 2 * BANK
 BANK_PASSES = K_BANK // K_PASS
 UNIT_BANKS = 2
 UNIT_PASSES = UNIT_BANKS * BANK_PASSES
-K_CHUNK = 4096
+INPUT1_CHUNKS = [4096, 8192, 8192]
+INPUT2_CHUNKS = [8192, 4096, 4096, 2048, 2048]
+K_CHUNK = max(INPUT1_CHUNKS + INPUT2_CHUNKS)
 CHUNK_PASSES = K_CHUNK // K_PASS
-CHUNKS = 2 * K_INPUT // K_CHUNK
-TAPER_CHUNKS = 2
-RAW_BUFS = 12
+RAW_BUFS = 8
 TRANSPOSE_BANKS = 6
 VECTOR_EVERY = 4
 RUN_BANKS = 6
@@ -40,7 +40,7 @@ FLOPS = 2 * X_BLOCKS * P * FEATURES * 2 * K_INPUT
 
 
 def chunk_list():
-    widths = [K_CHUNK] * (CHUNKS - TAPER_CHUNKS) + [K_CHUNK // 2] * (2 * TAPER_CHUNKS)
+    widths = INPUT1_CHUNKS + INPUT2_CHUNKS
     return [(sum(widths[:j]), width) for j, width in enumerate(widths)]
 
 
@@ -52,7 +52,7 @@ def tile_fcd_pa_kernel(tc, input1, input2, W1, b1, out):
         const = ctx.enter_context(tc.tile_pool(name="const", bufs=1))
         raw_pool = ctx.enter_context(tc.tile_pool(name="raw", bufs=RAW_BUFS))
         grouped_pool = ctx.enter_context(tc.tile_pool(name="grouped", bufs=4))
-        mx_pool = ctx.enter_context(tc.tile_pool(name="mx", bufs=3))
+        mx_pool = ctx.enter_context(tc.tile_pool(name="mx", bufs=2))
         tail = ctx.enter_context(tc.tile_pool(name="tail", bufs=1))
         bank_pool = ctx.enter_context(tc.psum_pool(name="banks", bufs=TRANSPOSE_BANKS))
         acc_pool = ctx.enter_context(tc.psum_pool(name="acc", bufs=1))

@@ -29,6 +29,7 @@ INPUT1_CHUNKS = [4096, 8192, 8192]
 INPUT2_CHUNKS = [8192, 4096, 4096, 2048, 2048]
 K_CHUNK = max(INPUT1_CHUNKS + INPUT2_CHUNKS)
 CHUNK_PASSES = K_CHUNK // K_PASS
+BIAS_CHUNK = 3
 RAW_BUFS = 8
 TRANSPOSE_BANKS = 6
 VECTOR_EVERY = 4
@@ -88,10 +89,12 @@ def tile_fcd_pa_kernel(tc, input1, input2, W1, b1, out):
 
         ones = const.tile([P, P], BF16)
         nc.vector.memset(ones[:], 1.0)
-        bias_bank = bank_pool.tile([P, BANK], F32, tag="bank")
-        nc.tensor.matmul(bias_bank[:, 0:FEATURES], lhsT=ones[:], rhs=bias_rows[:], start=True, stop=True)
         bias = const.tile([P, FEATURES], F32)
-        nc.vector.tensor_copy(out=bias[:], in_=bias_bank[:, 0:FEATURES])
+
+        def spread_bias():
+            bias_bank = bank_pool.tile([P, BANK], F32, tag="bank")
+            nc.tensor.matmul(bias_bank[:, 0:FEATURES], lhsT=ones[:], rhs=bias_rows[:], start=True, stop=True)
+            nc.vector.tensor_copy(out=bias[:], in_=bias_bank[:, 0:FEATURES])
 
         acc = [acc_pool.tile([P, FEATURES], F32, name="acc%d" % h) for h in range(X_BLOCKS)]
 
@@ -133,6 +136,8 @@ def tile_fcd_pa_kernel(tc, input1, input2, W1, b1, out):
         n = 0
         last = len(chunks) - 1
         for j in range(len(chunks)):
+            if j == BIAS_CHUNK:
+                spread_bias()
             codes = mx_pool.tile([P, BLOCKS * CHUNK_PASSES * P], U32, align_bytes=64)
             scales = mx_pool.tile([P, BLOCKS * CHUNK_PASSES * P], U8, align_bytes=64)
             packed[j] = (codes, scales)

@@ -25,12 +25,12 @@ K_BANK = 2 * BANK
 BANK_PASSES = K_BANK // K_PASS
 UNIT_BANKS = 2
 UNIT_PASSES = UNIT_BANKS * BANK_PASSES
-INPUT1_CHUNKS = [4096, 8192, 8192]
+INPUT1_CHUNKS = [10240, 10240]
 INPUT2_CHUNKS = [8192, 4096, 4096, 2048, 2048]
 K_CHUNK = max(INPUT1_CHUNKS + INPUT2_CHUNKS)
 CHUNK_PASSES = K_CHUNK // K_PASS
 BIAS_CHUNK = 3
-RAW_BUFS = 8
+RAW_BUFS = 6
 TRANSPOSE_BANKS = 6
 VECTOR_EVERY = 4
 RUN_BANKS = 6

@@ -24,7 +24,6 @@ BANK = 512
 K_BANK = 2 * BANK
 BANK_PASSES = K_BANK // K_PASS
 UNIT_BANKS = 2
-UNIT_PASSES = UNIT_BANKS * BANK_PASSES
 INPUT1_CHUNKS = [10240, 10240]
 INPUT2_CHUNKS = [8192, 4096, 4096, 2048, 2048]
 K_CHUNK = max(INPUT1_CHUNKS + INPUT2_CHUNKS)
@@ -71,11 +70,13 @@ def tile_fcd_pa_kernel(tc, input1, input2, W1, b1, out):
                 rows = W1[:, k0 : k0 + width]
             else:
                 source = input1 if k0 < K_INPUT else input2
-                first = k0 % K_INPUT
+                start = k0 % K_INPUT
                 h = block - X_FIRST
-                rows = source.rearrange("b o k -> b (o k)")[h * P : (h + 1) * P, first : first + width]
+                rows = source.rearrange("b o k -> b (o k)")[h * P : (h + 1) * P, start : start + width]
             raw[m] = raw_pool.tile([P, K_CHUNK], BF16, name="raw_tile")
-            nc.sync.dma_start(out=raw[m][:, 0:width], in_=rows)
+            step = K_BANK if m == BLOCKS * len(chunks) - 1 else width
+            for first in range(0, width, step):
+                nc.sync.dma_start(out=raw[m][:, first : first + step], in_=rows[:, first : first + step])
 
         for m in range(RAW_BUFS):
             load(m)
@@ -98,20 +99,22 @@ def tile_fcd_pa_kernel(tc, input1, input2, W1, b1, out):
 
         acc = [acc_pool.tile([P, FEATURES], F32, name="acc%d" % h) for h in range(X_BLOCKS)]
 
-        def transpose_bank(n, pairs, target):
+        def transpose_bank(on_vector, pairs, target):
             bank = bank_pool.tile([P, BANK], F32, tag="bank")
             for s in range(BANK // P):
                 nc.tensor.transpose(bank[:, s * P : (s + 1) * P], pairs[:, s * P : (s + 1) * P], ident[:])
             by_row = bank[:].rearrange("p (c u r) -> p c r u", c=BANK_PASSES, u=2)
             target_by_row = target.bitcast(F32).rearrange("p (c r u) -> p c r u", c=BANK_PASSES, u=2)
-            if n % VECTOR_EVERY == 0:
+            if on_vector:
                 nc.vector.tensor_copy(out=target_by_row, in_=by_row)
             else:
                 nc.scalar.copy(out=target_by_row, in_=by_row)
 
-        def quantise(grouped, codes, scales, first_word):
-            words = slice(first_word, first_word + UNIT_PASSES * P)
-            nc.vector.quantize_mx(out=codes[:, words].bitcast(FP8X4), scales=scales[:, words], in_=grouped[:])
+        def quantise(grouped, banks, codes, scales, first_word):
+            words = slice(first_word, first_word + banks * BANK_PASSES * P)
+            nc.vector.quantize_mx(
+                out=codes[:, words].bitcast(FP8X4), scales=scales[:, words], in_=grouped[:, 0 : banks * 2 * BANK]
+            )
 
         def multiply(j, passes, halves=range(X_BLOCKS)):
             codes, scales = packed[j]
@@ -149,19 +152,26 @@ def tile_fcd_pa_kernel(tc, input1, input2, W1, b1, out):
                 pairs = raw[m][:].bitcast(F32)
                 if j == last and block == BLOCKS - 1:
                     multiply(j - 1, range(chunks[j - 1][1] // K_PASS))
+                unit_banks = 1 if j == last and block == BLOCKS - 1 else UNIT_BANKS
                 for b in range(chunk_banks):
-                    half = b % UNIT_BANKS
-                    if half == 0:
+                    place = b % unit_banks
+                    if place == 0:
                         grouped = grouped_pool.tile([P, UNIT_BANKS * 2 * BANK], BF16, align_bytes=64)
+                    if j == last:
+                        on_vector = b == 0 and block != BLOCKS - 1
+                    else:
+                        on_vector = n % VECTOR_EVERY == 0
                     transpose_bank(
-                        n, pairs[:, b * BANK : (b + 1) * BANK], grouped[:, half * 2 * BANK : (half + 1) * 2 * BANK]
+                        on_vector,
+                        pairs[:, b * BANK : (b + 1) * BANK],
+                        grouped[:, place * 2 * BANK : (place + 1) * 2 * BANK],
                     )
                     n += 1
-                    if half == UNIT_BANKS - 1:
+                    if place == unit_banks - 1:
                         if waiting is not None:
                             quantise(*waiting)
-                        first_word = (block * CHUNK_PASSES + (b - half) * BANK_PASSES) * P
-                        waiting = (grouped, codes, scales, first_word)
+                        first_word = (block * CHUNK_PASSES + (b - place) * BANK_PASSES) * P
+                        waiting = (grouped, unit_banks, codes, scales, first_word)
                         if j == last:
                             quantise(*waiting)
                             waiting = None

@@ -23,7 +23,7 @@ K_PASS = P * PACK
 BANK = 512
 K_BANK = 2 * BANK
 BANK_PASSES = K_BANK // K_PASS
-UNIT_BANKS = 2
+UNIT_BANKS = 4
 INPUT1_CHUNKS = [10240, 10240]
 INPUT2_CHUNKS = [8192, 4096, 4096, 2048, 2048]
 K_CHUNK = max(INPUT1_CHUNKS + INPUT2_CHUNKS)
@@ -31,7 +31,7 @@ CHUNK_PASSES = K_CHUNK // K_PASS
 BIAS_CHUNK = 3
 RAW_BUFS = 6
 TRANSPOSE_BANKS = 6
-VECTOR_EVERY = 4
+VECTOR_EVERY = 5
 RUN_BANKS = 6
 EPS = 1e-5
 SLOPE = 0.2
@@ -51,7 +51,7 @@ def tile_fcd_pa_kernel(tc, input1, input2, W1, b1, out):
         ctx.enter_context(tc.manual_schedule())
         const = ctx.enter_context(tc.tile_pool(name="const", bufs=1))
         raw_pool = ctx.enter_context(tc.tile_pool(name="raw", bufs=RAW_BUFS))
-        grouped_pool = ctx.enter_context(tc.tile_pool(name="grouped", bufs=4))
+        grouped_pool = ctx.enter_context(tc.tile_pool(name="grouped", bufs=3))
         mx_pool = ctx.enter_context(tc.tile_pool(name="mx", bufs=2))
         tail = ctx.enter_context(tc.tile_pool(name="tail", bufs=1))
         bank_pool = ctx.enter_context(tc.psum_pool(name="banks", bufs=TRANSPOSE_BANKS))
@@ -167,11 +167,11 @@ def tile_fcd_pa_kernel(tc, input1, input2, W1, b1, out):
                         grouped[:, place * 2 * BANK : (place + 1) * 2 * BANK],
                     )
                     n += 1
-                    if place == unit_banks - 1:
+                    if place == unit_banks - 1 or b == chunk_banks - 1:
                         if waiting is not None:
                             quantise(*waiting)
                         first_word = (block * CHUNK_PASSES + (b - place) * BANK_PASSES) * P
-                        waiting = (grouped, unit_banks, codes, scales, first_word)
+                        waiting = (grouped, place + 1, codes, scales, first_word)
                         if j == last:
                             quantise(*waiting)
                             waiting = None

@@ -23,9 +23,9 @@ K_PASS = P * PACK
 BANK = 512
 K_BANK = 2 * BANK
 BANK_PASSES = K_BANK // K_PASS
-UNIT_BANKS = 4
+UNIT_BANKS = 2
 INPUT1_CHUNKS = [10240, 10240]
-INPUT2_CHUNKS = [8192, 4096, 4096, 2048, 2048]
+INPUT2_CHUNKS = [6144, 6144, 4096, 2048, 2048]
 K_CHUNK = max(INPUT1_CHUNKS + INPUT2_CHUNKS)
 CHUNK_PASSES = K_CHUNK // K_PASS
 BIAS_CHUNK = 3
@@ -33,6 +33,8 @@ RAW_BUFS = 6
 TRANSPOSE_BANKS = 6
 VECTOR_EVERY = 5
 RUN_BANKS = 6
+RUN_MATMULS = 8
+SMALL_CHUNK = 4096
 EPS = 1e-5
 SLOPE = 0.2
 
@@ -51,7 +53,7 @@ def tile_fcd_pa_kernel(tc, input1, input2, W1, b1, out):
         ctx.enter_context(tc.manual_schedule())
         const = ctx.enter_context(tc.tile_pool(name="const", bufs=1))
         raw_pool = ctx.enter_context(tc.tile_pool(name="raw", bufs=RAW_BUFS))
-        grouped_pool = ctx.enter_context(tc.tile_pool(name="grouped", bufs=3))
+        grouped_pool = ctx.enter_context(tc.tile_pool(name="grouped", bufs=4))
         mx_pool = ctx.enter_context(tc.tile_pool(name="mx", bufs=2))
         tail = ctx.enter_context(tc.tile_pool(name="tail", bufs=1))
         bank_pool = ctx.enter_context(tc.psum_pool(name="banks", bufs=TRANSPOSE_BANKS))
@@ -61,25 +63,37 @@ def tile_fcd_pa_kernel(tc, input1, input2, W1, b1, out):
         nc.vector.memset(bias_rows[:], 0.0)
         nc.scalar.dma_start(out=bias_rows[0:1, :], in_=b1.rearrange("(o f) -> o f", o=1))
 
+        tiles = [(j, block) for j in range(len(chunks)) for block in range(BLOCKS)]
+        groups = []
+        used = K_CHUNK
+        for m, (j, block) in enumerate(tiles):
+            width = chunks[j][1]
+            if used + width > K_CHUNK:
+                groups.append([])
+                used = 0
+            groups[-1].append((m, used))
+            used += width
         raw = {}
 
-        def load(m):
-            k0, width = chunks[m // BLOCKS]
-            block = m % BLOCKS
-            if block == W_BLOCK:
-                rows = W1[:, k0 : k0 + width]
-            else:
-                source = input1 if k0 < K_INPUT else input2
-                start = k0 % K_INPUT
-                h = block - X_FIRST
-                rows = source.rearrange("b o k -> b (o k)")[h * P : (h + 1) * P, start : start + width]
-            raw[m] = raw_pool.tile([P, K_CHUNK], BF16, name="raw_tile")
-            step = K_BANK if m == BLOCKS * len(chunks) - 1 else width
-            for first in range(0, width, step):
-                nc.sync.dma_start(out=raw[m][:, first : first + step], in_=rows[:, first : first + step])
+        def load(group):
+            buffer = raw_pool.tile([P, K_CHUNK], BF16, name="raw_buffer")
+            for m, column in group:
+                j, block = tiles[m]
+                k0, width = chunks[j]
+                if block == W_BLOCK:
+                    rows = W1[:, k0 : k0 + width]
+                else:
+                    source = input1 if k0 < K_INPUT else input2
+                    start = k0 % K_INPUT
+                    h = block - X_FIRST
+                    rows = source.rearrange("b o k -> b (o k)")[h * P : (h + 1) * P, start : start + width]
+                raw[m] = buffer[:, column : column + width]
+                step = K_BANK if m == len(tiles) - 1 else width
+                for first in range(0, width, step):
+                    nc.sync.dma_start(out=raw[m][:, first : first + step], in_=rows[:, first : first + step])
 
-        for m in range(RAW_BUFS):
-            load(m)
+        for group in groups[0:RAW_BUFS]:
+            load(group)
 
         one = const.tile([P, 1], F32)
         nc.vector.memset(one[:], 1.0)
@@ -110,50 +124,62 @@ def tile_fcd_pa_kernel(tc, input1, input2, W1, b1, out):
             else:
                 nc.scalar.copy(out=target_by_row, in_=by_row)
 
-        def quantise(grouped, banks, codes, scales, first_word):
-            words = slice(first_word, first_word + banks * BANK_PASSES * P)
+        def multiply(j, h, c):
+            codes, scales = packed[j]
+            x_slot = (X_FIRST + h) * CHUNK_PASSES + c
+            x_words = slice(x_slot * P, (x_slot + 1) * P)
+            w_words = slice((W_BLOCK * CHUNK_PASSES + c) * P, (W_BLOCK * CHUNK_PASSES + c + 1) * P)
+            nc.tensor.matmul_mx(
+                out=acc[h][:],
+                lhsT=codes[:, x_words].bitcast(FP8X4),
+                lhsT_scale=scales[:, x_words],
+                rhs=codes[:, w_words].bitcast(FP8X4),
+                rhs_scale=scales[:, w_words],
+                start=(j == 0 and c == 0),
+                stop=(j == last and c == chunks[j][1] // K_PASS - 1),
+            )
+
+        last = len(chunks) - 1
+        packed = {}
+        waiting = None
+        ready = []
+        fresh = []
+        n = 0
+
+        def quantise(grouped, j, block, first_bank, banks):
+            codes, scales = packed[j]
+            first_pass = first_bank * BANK_PASSES
+            first_slot = block * CHUNK_PASSES + first_pass
+            words = slice(first_slot * P, (first_slot + banks * BANK_PASSES) * P)
             nc.vector.quantize_mx(
                 out=codes[:, words].bitcast(FP8X4), scales=scales[:, words], in_=grouped[:, 0 : banks * 2 * BANK]
             )
+            if block != W_BLOCK:
+                for c in range(first_pass, first_pass + banks * BANK_PASSES):
+                    fresh.append((j, block - X_FIRST, c))
 
-        def multiply(j, passes, halves=range(X_BLOCKS)):
-            codes, scales = packed[j]
-            last_pass = chunks[j][1] // K_PASS - 1
-            for h in halves:
-                for c in passes:
-                    x_slot = (X_FIRST + h) * CHUNK_PASSES + c
-                    x_words = slice(x_slot * P, (x_slot + 1) * P)
-                    w_words = slice((W_BLOCK * CHUNK_PASSES + c) * P, (W_BLOCK * CHUNK_PASSES + c + 1) * P)
-                    nc.tensor.matmul_mx(
-                        out=acc[h][:],
-                        lhsT=codes[:, x_words].bitcast(FP8X4),
-                        lhsT_scale=scales[:, x_words],
-                        rhs=codes[:, w_words].bitcast(FP8X4),
-                        rhs_scale=scales[:, w_words],
-                        start=(j == 0 and c == 0),
-                        stop=(j == len(chunks) - 1 and c == last_pass),
-                    )
+        def run(most):
+            for pass_of_x in ready[0:most]:
+                multiply(*pass_of_x)
+            left = ready[most:] + fresh
+            ready.clear()
+            ready.extend(left)
+            fresh.clear()
 
-        packed = {}
-        waiting = None
-        n = 0
-        last = len(chunks) - 1
         for j in range(len(chunks)):
             if j == BIAS_CHUNK:
                 spread_bias()
+            width = chunks[j][1]
             codes = mx_pool.tile([P, BLOCKS * CHUNK_PASSES * P], U32, align_bytes=64)
             scales = mx_pool.tile([P, BLOCKS * CHUNK_PASSES * P], U8, align_bytes=64)
             packed[j] = (codes, scales)
-            chunk_banks = chunks[j][1] // K_BANK
-            runs = BLOCKS * chunk_banks // RUN_BANKS
-            share = chunks[j - 1][1] // K_PASS // runs if j > 0 else 0
             for block in range(BLOCKS):
                 m = j * BLOCKS + block
-                pairs = raw[m][:].bitcast(F32)
-                if j == last and block == BLOCKS - 1:
-                    multiply(j - 1, range(chunks[j - 1][1] // K_PASS))
+                pairs = raw[m].bitcast(F32)
+                if j == last and block > W_BLOCK:
+                    run(len(ready))
                 unit_banks = 1 if j == last and block == BLOCKS - 1 else UNIT_BANKS
-                for b in range(chunk_banks):
+                for b in range(width // K_BANK):
                     place = b % unit_banks
                     if place == 0:
                         grouped = grouped_pool.tile([P, UNIT_BANKS * 2 * BANK], BF16, align_bytes=64)
@@ -167,22 +193,21 @@ def tile_fcd_pa_kernel(tc, input1, input2, W1, b1, out):
                         grouped[:, place * 2 * BANK : (place + 1) * 2 * BANK],
                     )
                     n += 1
-                    if place == unit_banks - 1 or b == chunk_banks - 1:
+                    if place == unit_banks - 1:
                         if waiting is not None:
                             quantise(*waiting)
-                        first_word = (block * CHUNK_PASSES + (b - place) * BANK_PASSES) * P
-                        waiting = (grouped, place + 1, codes, scales, first_word)
+                        waiting = (grouped, j, block, b - place, unit_banks)
                         if j == last:
                             quantise(*waiting)
                             waiting = None
-                    done = block * chunk_banks + b + 1
-                    if 0 < j < last and done % RUN_BANKS == 0:
-                        run = done // RUN_BANKS
-                        multiply(j - 1, range((run - 1) * share, run * share))
-                if m + RAW_BUFS < BLOCKS * len(chunks):
-                    load(m + RAW_BUFS)
-        for h in range(X_BLOCKS):
-            multiply(last, range(chunks[last][1] // K_PASS), halves=[h])
+                    if n % RUN_BANKS == 0 and j < last:
+                        run(RUN_MATMULS if width > SMALL_CHUNK else len(ready))
+                if m == groups[0][-1][0]:
+                    groups = groups[1:]
+                    if len(groups) >= RAW_BUFS:
+                        load(groups[RAW_BUFS - 1])
+        run(len(ready))
+        run(len(ready))
 
         h_sb = tail.tile([P, X_BLOCKS, FEATURES], F32)
         stats = tail.tile([P, X_BLOCKS, 6], F32)

@@ -25,7 +25,7 @@ K_BANK = 2 * BANK
 BANK_PASSES = K_BANK // K_PASS
 UNIT_BANKS = 2
 INPUT1_CHUNKS = [10240, 10240]
-INPUT2_CHUNKS = [6144, 6144, 4096, 2048, 2048]
+INPUT2_CHUNKS = [6144, 6144, 4096, 4096]
 K_CHUNK = max(INPUT1_CHUNKS + INPUT2_CHUNKS)
 CHUNK_PASSES = K_CHUNK // K_PASS
 BIAS_CHUNK = 3
@@ -34,7 +34,7 @@ TRANSPOSE_BANKS = 6
 VECTOR_EVERY = 5
 RUN_BANKS = 6
 RUN_MATMULS = 8
-SMALL_CHUNK = 4096
+SMALL_CHUNK = 10240
 EPS = 1e-5
 SLOPE = 0.2
 
@@ -88,9 +88,11 @@ def tile_fcd_pa_kernel(tc, input1, input2, W1, b1, out):
                     h = block - X_FIRST
                     rows = source.rearrange("b o k -> b (o k)")[h * P : (h + 1) * P, start : start + width]
                 raw[m] = buffer[:, column : column + width]
-                step = K_BANK if m == len(tiles) - 1 else width
-                for first in range(0, width, step):
-                    nc.sync.dma_start(out=raw[m][:, first : first + step], in_=rows[:, first : first + step])
+                cuts = [0, width]
+                if m == len(tiles) - 1:
+                    cuts = [0, width - 2 * K_BANK, width - K_BANK, width]
+                for first, end in zip(cuts[:-1], cuts[1:]):
+                    nc.sync.dma_start(out=raw[m][:, first:end], in_=rows[:, first:end])
 
         for group in groups[0:RAW_BUFS]:
             load(group)
@@ -212,8 +214,7 @@ def tile_fcd_pa_kernel(tc, input1, input2, W1, b1, out):
         h_sb = tail.tile([P, X_BLOCKS, FEATURES], F32)
         stats = tail.tile([P, X_BLOCKS, 6], F32)
         mean_var = tail.tile([P, X_BLOCKS, 2], F32)
-        centred = tail.tile([P, X_BLOCKS, FEATURES], F32)
-        leaky = tail.tile([P, X_BLOCKS, FEATURES], F32)
+        normed = tail.tile([P, X_BLOCKS, FEATURES], F32)
         rstd = [tail.tile([P, 1], F32, name="rstd%d" % h) for h in range(X_BLOCKS)]
         result = [tail.tile([P, FEATURES], F32, name="result%d" % h) for h in range(X_BLOCKS)]
 
@@ -229,32 +230,34 @@ def tile_fcd_pa_kernel(tc, input1, input2, W1, b1, out):
                 out=rstd[h][:], in_=mean_var[:, h, 1:2], func=ACT.Abs_reciprocal_sqrt, bias=EPS, scale=1.0
             )
 
-        def centre(h):
-            nc.vector.tensor_scalar_sub(out=centred[:, h, :], in0=h_sb[:, h, :], scalar1=mean_var[:, h, 0:1])
-
-        def relu(h):
-            nc.vector.scalar_tensor_tensor(
-                out=leaky[:, h, :],
-                in0=centred[:, h, :],
-                scalar=SLOPE,
-                in1=centred[:, h, :],
-                op0=ALU.mult,
-                op1=ALU.max,
+        def normalise(h):
+            nc.vector.tensor_scalar(
+                out=normed[:, h, :],
+                in0=h_sb[:, h, :],
+                scalar1=mean_var[:, h, 0:1],
+                scalar2=rstd[h][:],
+                op0=ALU.subtract,
+                op1=ALU.mult,
             )
 
         def store(h, queue):
-            nc.vector.tensor_scalar_mul(out=result[h][:], in0=leaky[:, h, :], scalar1=rstd[h][:])
+            nc.vector.scalar_tensor_tensor(
+                out=result[h][:],
+                in0=normed[:, h, :],
+                scalar=SLOPE,
+                in1=normed[:, h, :],
+                op0=ALU.mult,
+                op1=ALU.max,
+            )
             queue.dma_start(out=out.rearrange("b o f -> b (o f)")[h * P : (h + 1) * P, :], in_=result[h][:])
 
         add_bias(0)
         take_stats(0)
-        take_mean_var(0)
         add_bias(1)
-        centre(0)
+        take_mean_var(0)
         take_stats(1)
-        relu(0)
+        normalise(0)
         take_mean_var(1)
         store(0, nc.scalar)
-        centre(1)
-        relu(1)
+        normalise(1)
         store(1, nc.sync)

from contextlib import ExitStack

import concourse.mybir as mybir
from concourse.masks import make_identity

F32 = mybir.dt.float32
BF16 = mybir.dt.bfloat16
U32 = mybir.dt.uint32
U8 = mybir.dt.uint8
FP8X4 = mybir.dt.float8_e4m3fn_x4
ALU = mybir.AluOpType
ACT = mybir.ActivationFunctionType

P = 128
X_BLOCKS = 2
BLOCKS = X_BLOCKS + 1
W_BLOCK = 0
X_FIRST = 1
FEATURES = 128
K_INPUT = 20480
PACK = 4
K_PASS = P * PACK
BANK = 512
K_BANK = 2 * BANK
BANK_PASSES = K_BANK // K_PASS
UNIT_BANKS = 2
INPUT1_CHUNKS = [10240, 10240]
INPUT2_CHUNKS = [6144, 6144, 4096, 4096]
K_CHUNK = max(INPUT1_CHUNKS + INPUT2_CHUNKS)
CHUNK_PASSES = K_CHUNK // K_PASS
BIAS_CHUNK = 3
RAW_BUFS = 6
TRANSPOSE_BANKS = 6
VECTOR_EVERY = 5
RUN_BANKS = 6
RUN_MATMULS = 8
SMALL_CHUNK = 10240
EPS = 1e-5
SLOPE = 0.2

FLOPS = 2 * X_BLOCKS * P * FEATURES * 2 * K_INPUT


def chunk_list():
    widths = INPUT1_CHUNKS + INPUT2_CHUNKS
    return [(sum(widths[:j]), width) for j, width in enumerate(widths)]


def tile_fcd_pa_kernel(tc, input1, input2, W1, b1, out):
    nc = tc.nc
    chunks = chunk_list()
    with ExitStack() as ctx:
        ctx.enter_context(tc.manual_schedule())
        const = ctx.enter_context(tc.tile_pool(name="const", bufs=1))
        raw_pool = ctx.enter_context(tc.tile_pool(name="raw", bufs=RAW_BUFS))
        grouped_pool = ctx.enter_context(tc.tile_pool(name="grouped", bufs=4))
        mx_pool = ctx.enter_context(tc.tile_pool(name="mx", bufs=2))
        tail = ctx.enter_context(tc.tile_pool(name="tail", bufs=1))
        bank_pool = ctx.enter_context(tc.psum_pool(name="banks", bufs=TRANSPOSE_BANKS))
        acc_pool = ctx.enter_context(tc.psum_pool(name="acc", bufs=1))

        bias_rows = const.tile([P, FEATURES], BF16)
        nc.vector.memset(bias_rows[:], 0.0)
        nc.scalar.dma_start(out=bias_rows[0:1, :], in_=b1.rearrange("(o f) -> o f", o=1))

        tiles = [(j, block) for j in range(len(chunks)) for block in range(BLOCKS)]
        groups = []
        used = K_CHUNK
        for m, (j, block) in enumerate(tiles):
            width = chunks[j][1]
            if used + width > K_CHUNK:
                groups.append([])
                used = 0
            groups[-1].append((m, used))
            used += width
        raw = {}

        def load(group):
            buffer = raw_pool.tile([P, K_CHUNK], BF16, name="raw_buffer")
            for m, column in group:
                j, block = tiles[m]
                k0, width = chunks[j]
                if block == W_BLOCK:
                    rows = W1[:, k0 : k0 + width]
                else:
                    source = input1 if k0 < K_INPUT else input2
                    start = k0 % K_INPUT
                    h = block - X_FIRST
                    rows = source.rearrange("b o k -> b (o k)")[h * P : (h + 1) * P, start : start + width]
                raw[m] = buffer[:, column : column + width]
                cuts = [0, width]
                if m == len(tiles) - 1:
                    cuts = [0, width - 2 * K_BANK, width - K_BANK, width]
                for first, end in zip(cuts[:-1], cuts[1:]):
                    nc.sync.dma_start(out=raw[m][:, first:end], in_=rows[:, first:end])

        for group in groups[0:RAW_BUFS]:
            load(group)

        one = const.tile([P, 1], F32)
        nc.vector.memset(one[:], 1.0)
        table_warmer = const.tile([P, 1], F32)
        nc.scalar.activation(out=table_warmer[:], in_=one[:], func=ACT.Abs_reciprocal_sqrt)
        ident = const.tile([P, P], F32)
        make_identity(nc, ident[:])

        ones = const.tile([P, P], BF16)
        nc.vector.memset(ones[:], 1.0)
        bias = const.tile([P, FEATURES], F32)

        def spread_bias():
            bias_bank = bank_pool.tile([P, BANK], F32, tag="bank")
            nc.tensor.matmul(bias_bank[:, 0:FEATURES], lhsT=ones[:], rhs=bias_rows[:], start=True, stop=True)
            nc.vector.tensor_copy(out=bias[:], in_=bias_bank[:, 0:FEATURES])

        acc = [acc_pool.tile([P, FEATURES], F32, name="acc%d" % h) for h in range(X_BLOCKS)]

        def transpose_bank(on_vector, pairs, target):
            bank = bank_pool.tile([P, BANK], F32, tag="bank")
            for s in range(BANK // P):
                nc.tensor.transpose(bank[:, s * P : (s + 1) * P], pairs[:, s * P : (s + 1) * P], ident[:])
            by_row = bank[:].rearrange("p (c u r) -> p c r u", c=BANK_PASSES, u=2)
            target_by_row = target.bitcast(F32).rearrange("p (c r u) -> p c r u", c=BANK_PASSES, u=2)
            if on_vector:
                nc.vector.tensor_copy(out=target_by_row, in_=by_row)
            else:
                nc.scalar.copy(out=target_by_row, in_=by_row)

        def multiply(j, h, c):
            codes, scales = packed[j]
            x_slot = (X_FIRST + h) * CHUNK_PASSES + c
            x_words = slice(x_slot * P, (x_slot + 1) * P)
            w_words = slice((W_BLOCK * CHUNK_PASSES + c) * P, (W_BLOCK * CHUNK_PASSES + c + 1) * P)
            nc.tensor.matmul_mx(
                out=acc[h][:],
                lhsT=codes[:, x_words].bitcast(FP8X4),
                lhsT_scale=scales[:, x_words],
                rhs=codes[:, w_words].bitcast(FP8X4),
                rhs_scale=scales[:, w_words],
                start=(j == 0 and c == 0),
                stop=(j == last and c == chunks[j][1] // K_PASS - 1),
            )

        last = len(chunks) - 1
        packed = {}
        waiting = None
        ready = []
        fresh = []
        n = 0

        def quantise(grouped, j, block, first_bank, banks):
            codes, scales = packed[j]
            first_pass = first_bank * BANK_PASSES
            first_slot = block * CHUNK_PASSES + first_pass
            words = slice(first_slot * P, (first_slot + banks * BANK_PASSES) * P)
            nc.vector.quantize_mx(
                out=codes[:, words].bitcast(FP8X4), scales=scales[:, words], in_=grouped[:, 0 : banks * 2 * BANK]
            )
            if block != W_BLOCK:
                for c in range(first_pass, first_pass + banks * BANK_PASSES):
                    fresh.append((j, block - X_FIRST, c))

        def run(most):
            for pass_of_x in ready[0:most]:
                multiply(*pass_of_x)
            left = ready[most:] + fresh
            ready.clear()
            ready.extend(left)
            fresh.clear()

        for j in range(len(chunks)):
            if j == BIAS_CHUNK:
                spread_bias()
            width = chunks[j][1]
            codes = mx_pool.tile([P, BLOCKS * CHUNK_PASSES * P], U32, align_bytes=64)
            scales = mx_pool.tile([P, BLOCKS * CHUNK_PASSES * P], U8, align_bytes=64)
            packed[j] = (codes, scales)
            for block in range(BLOCKS):
                m = j * BLOCKS + block
                pairs = raw[m].bitcast(F32)
                if j == last and block > W_BLOCK:
                    run(len(ready))
                unit_banks = 1 if j == last and block == BLOCKS - 1 else UNIT_BANKS
                for b in range(width // K_BANK):
                    place = b % unit_banks
                    if place == 0:
                        grouped = grouped_pool.tile([P, UNIT_BANKS * 2 * BANK], BF16, align_bytes=64)
                    if j == last:
                        on_vector = b == 0 and block != BLOCKS - 1
                    else:
                        on_vector = n % VECTOR_EVERY == 0
                    transpose_bank(
                        on_vector,
                        pairs[:, b * BANK : (b + 1) * BANK],
                        grouped[:, place * 2 * BANK : (place + 1) * 2 * BANK],
                    )
                    n += 1
                    if place == unit_banks - 1:
                        if waiting is not None:
                            quantise(*waiting)
                        waiting = (grouped, j, block, b - place, unit_banks)
                        if j == last:
                            quantise(*waiting)
                            waiting = None
                    if n % RUN_BANKS == 0 and j < last:
                        run(RUN_MATMULS if width > SMALL_CHUNK else len(ready))
                if m == groups[0][-1][0]:
                    groups = groups[1:]
                    if len(groups) >= RAW_BUFS:
                        load(groups[RAW_BUFS - 1])
        run(len(ready))
        run(len(ready))

        h_sb = tail.tile([P, X_BLOCKS, FEATURES], F32)
        stats = tail.tile([P, X_BLOCKS, 6], F32)
        mean_var = tail.tile([P, X_BLOCKS, 2], F32)
        normed = tail.tile([P, X_BLOCKS, FEATURES], F32)
        rstd = [tail.tile([P, 1], F32, name="rstd%d" % h) for h in range(X_BLOCKS)]
        result = [tail.tile([P, FEATURES], F32, name="result%d" % h) for h in range(X_BLOCKS)]

        def add_bias(h):
            nc.vector.tensor_tensor(out=h_sb[:, h, :], in0=acc[h][:], in1=bias[:], op=ALU.add)

        def take_stats(h):
            nc.vector.bn_stats(out=stats[:, h, :], in_=h_sb[:, h, :])

        def take_mean_var(h):
            nc.vector.bn_aggr(out=mean_var[:, h, :], in_=stats[:, h, :])
            nc.scalar.activation(
                out=rstd[h][:], in_=mean_var[:, h, 1:2], func=ACT.Abs_reciprocal_sqrt, bias=EPS, scale=1.0
            )

        def normalise(h):
            nc.vector.tensor_scalar(
                out=normed[:, h, :],
                in0=h_sb[:, h, :],
                scalar1=mean_var[:, h, 0:1],
                scalar2=rstd[h][:],
                op0=ALU.subtract,
                op1=ALU.mult,
            )

        def store(h, queue):
            nc.vector.scalar_tensor_tensor(
                out=result[h][:],
                in0=normed[:, h, :],
                scalar=SLOPE,
                in1=normed[:, h, :],
                op0=ALU.mult,
                op1=ALU.max,
            )
            queue.dma_start(out=out.rearrange("b o f -> b (o f)")[h * P : (h + 1) * P, :], in_=result[h][:])

        add_bias(0)
        take_stats(0)
        add_bias(1)
        take_mean_var(0)
        take_stats(1)
        normalise(0)
        take_mean_var(1)
        store(0, nc.scalar)
        normalise(1)
        store(1, nc.sync)
